import numpy as np
import ml_dtypes

BF16 = ml_dtypes.bfloat16


def bf(x):
    return np.asarray(x, np.float32).astype(BF16)


def f32(x):
    return np.asarray(x, np.float32)


def f64(x):
    return np.asarray(x).astype(np.float64)


def striped(idx):
    return np.tile(idx.reshape(-1, 16).T, (8, 1))


D, S, H, FI, FO, R, N = 128, 512, 128, 128, 128, 2, 1024
ALPHA = 1.0


def silu(v):
    return v / (1.0 + np.exp(-v))


def setup_inputs():
    return {
        "styles": bf(np.random.standard_normal((D, S))),
        "w1": bf(np.random.standard_normal((D, H)) / np.sqrt(D)),
        "b1": f32(0.1 * np.random.standard_normal((H, 1))),
        "w2": bf(0.5 * np.random.standard_normal((H, (FI + FO) * R)) / np.sqrt(H)),
        "b2": f32(0.1 * np.random.standard_normal(((FI + FO) * R, 1))),
        "x": bf(np.random.standard_normal((FI, N))),
        "wb": bf(np.random.standard_normal((FI, FO)) / np.sqrt(FI)),
        "bb": f32(0.1 * np.random.standard_normal((FO, 1))),
        "offs": striped(np.random.permutation(np.tile(np.arange(S), 2))[:N]),
    }


def reference(styles, w1, b1, w2, b2, x, wb, bb, offs):
    idx = offs[:16].T.reshape(-1)
    h = silu(f64(w1).T @ f64(styles)[:, idx] + f64(b1))
    p = f64(w2).T @ h + f64(b2)
    a = p[:FI * R].reshape(R, FI, N)
    bm = p[FI * R:].reshape(R, FO, N)
    low = (a * f64(x)[None]).sum(axis=1)
    delta = (low[:, None, :] * bm).sum(axis=0)
    return f64(wb).T @ f64(x) + f64(bb) + ALPHA * delta

@@ -1,0 +1,82 @@
+import concourse.mybir as mybir
+
+P = 128
+S = 512
+N = 1024
+R = 2
+PIECE = 512
+BF16, F32, U16 = mybir.dt.bfloat16, mybir.dt.float32, mybir.dt.uint16
+ADD, MULT = mybir.AluOpType.add, mybir.AluOpType.mult
+SILU, IDENTITY = mybir.ActivationFunctionType.Silu, mybir.ActivationFunctionType.Identity
+
+FLOPS = 2 * N * (P * P + P * 2 * R * P + P * P) + 4 * R * P * N
+
+
+def tile_stylehyperlinear_kernel(tc, styles, w1, b1, w2, b2, x, wb, bb, offs, out):
+    nc = tc.nc
+    with (
+        tc.tile_pool(name="held", bufs=1) as held,
+        tc.tile_pool(name="work", bufs=2) as work,
+        tc.psum_pool(name="psum", bufs=8) as psum,
+    ):
+        offsets = held.tile([P, N // 16], U16, name="offsets")
+        nc.sync.dma_start(offsets[:], offs)
+        bank = held.tile([P, S], BF16, name="bank")
+        nc.sync.dma_start(bank[:], styles)
+        w1_sb = held.tile([P, P], BF16, name="w1_sb")
+        nc.scalar.dma_start(w1_sb[:], w1)
+        b1_sb = held.tile([P, 1], F32, name="b1_sb")
+        nc.scalar.dma_start(b1_sb[:], b1)
+        w2_sb = held.tile([P, 2 * R * P], BF16, name="w2_sb")
+        nc.sync.dma_start(w2_sb[:], w2)
+        x_sb = held.tile([P, N], BF16, name="x_sb")
+        nc.scalar.dma_start(x_sb[:], x)
+        b2_sb = held.tile([P, 2 * R], F32, name="b2_sb")
+        with nc.allow_non_contiguous_dma(reason="512 biases, one to a partition and block"):
+            nc.scalar.dma_start(b2_sb[:], b2.rearrange("(q p) one -> p (q one)", p=P))
+        wb_sb = held.tile([P, P], BF16, name="wb_sb")
+        nc.sync.dma_start(wb_sb[:], wb)
+        bb_sb = held.tile([P, 1], F32, name="bb_sb")
+        nc.scalar.dma_start(bb_sb[:], bb)
+        ones = held.tile([P, P], BF16, name="ones")
+        nc.vector.memset(ones[:], 1.0)
+
+        z_pieces = []
+        for c in range(N // PIECE):
+            z = psum.tile([P, PIECE], F32, name=f"z{c}", tag="bank")
+            looked_up = bank[:].indirect(offsets[:, c * (PIECE // 16) : (c + 1) * (PIECE // 16)])
+            nc.tensor.matmul(z[:], w1_sb[:], looked_up, start=True, stop=True)
+            z_pieces.append(z)
+
+        for c in range(N // PIECE):
+            cols = slice(c * PIECE, (c + 1) * PIECE)
+            h = work.tile([P, PIECE], BF16, name="h")
+            nc.scalar.activation(h[:], z_pieces[c][:], SILU, bias=b1_sb[:])
+
+            p_blocks = []
+            for q in range(2 * R):
+                p_q = psum.tile([P, PIECE], F32, name=f"p{q}", tag="bank")
+                nc.tensor.matmul(p_q[:], w2_sb[:, q * P : (q + 1) * P], h[:], start=True, stop=True)
+                p_blocks.append(p_q)
+            base = psum.tile([P, PIECE], F32, name="base", tag="bank")
+            nc.tensor.matmul(base[:], wb_sb[:], x_sb[:, cols], start=True, stop=True)
+
+            terms = []
+            for r in range(R):
+                prod = work.tile([P, PIECE], BF16, name=f"prod{r}")
+                nc.vector.scalar_tensor_tensor(
+                    prod[:], p_blocks[r][:], b2_sb[:, r : r + 1], x_sb[:, cols], op0=ADD, op1=MULT
+                )
+                low = psum.tile([P, PIECE], F32, name=f"low{r}", tag="bank")
+                nc.tensor.matmul(low[:], ones[:], prod[:], start=True, stop=True)
+                vec = work.tile([P, PIECE], F32, name=f"vec{r}")
+                nc.scalar.activation(vec[:], p_blocks[R + r][:], IDENTITY, bias=b2_sb[:, R + r : R + r + 1])
+                term = work.tile([P, PIECE], F32, name=f"term{r}")
+                nc.vector.tensor_tensor(term[:], low[:], vec[:], MULT)
+                terms.append(term)
+
+            part = work.tile([P, PIECE], F32, name="part")
+            nc.vector.scalar_tensor_tensor(part[:], base[:], bb_sb[:], terms[0][:], op0=ADD, op1=ADD)
+            res = work.tile([P, PIECE], F32, name="res")
+            nc.vector.tensor_tensor(res[:], part[:], terms[1][:], ADD)
+            nc.sync.dma_start(out[:, cols], res[:])

@@ -1,10 +1,14 @@
 import concourse.mybir as mybir
+from concourse.masks import make_identity
 
 P = 128
 S = 512
 N = 1024
 R = 2
 PIECE = 512
+CHUNK = 256
+WARM_UP = 4
+N_BIAS = 2 + 2 * R
 BF16, F32, U16 = mybir.dt.bfloat16, mybir.dt.float32, mybir.dt.uint16
 ADD, MULT = mybir.AluOpType.add, mybir.AluOpType.mult
 SILU, IDENTITY = mybir.ActivationFunctionType.Silu, mybir.ActivationFunctionType.Identity
@@ -16,30 +20,44 @@ def tile_stylehyperlinear_kernel(tc, styles, w1, b1, w2, b2, x, wb, bb, offs, ou
     nc = tc.nc
     with (
         tc.tile_pool(name="held", bufs=1) as held,
-        tc.tile_pool(name="work", bufs=2) as work,
+        tc.tile_pool(name="work", bufs=N // CHUNK) as work,
         tc.psum_pool(name="psum", bufs=8) as psum,
     ):
         offsets = held.tile([P, N // 16], U16, name="offsets")
         nc.sync.dma_start(offsets[:], offs)
-        bank = held.tile([P, S], BF16, name="bank")
-        nc.sync.dma_start(bank[:], styles)
         w1_sb = held.tile([P, P], BF16, name="w1_sb")
         nc.scalar.dma_start(w1_sb[:], w1)
-        b1_sb = held.tile([P, 1], F32, name="b1_sb")
-        nc.scalar.dma_start(b1_sb[:], b1)
+        bank = held.tile([P, S], BF16, name="bank")
+        nc.sync.dma_start(bank[:], styles)
+        bias_rows = held.tile([N_BIAS, P], F32, name="bias_rows")
+        nc.scalar.dma_start(bias_rows[0:1, :], b1.rearrange("p one -> one p"))
+        nc.scalar.dma_start(bias_rows[1 : 1 + 2 * R, :], b2.rearrange("(q p) one -> q (p one)", p=P))
+        nc.scalar.dma_start(bias_rows[1 + 2 * R : N_BIAS, :], bb.rearrange("p one -> one p"))
         w2_sb = held.tile([P, 2 * R * P], BF16, name="w2_sb")
         nc.sync.dma_start(w2_sb[:], w2)
-        x_sb = held.tile([P, N], BF16, name="x_sb")
-        nc.scalar.dma_start(x_sb[:], x)
-        b2_sb = held.tile([P, 2 * R], F32, name="b2_sb")
-        with nc.allow_non_contiguous_dma(reason="512 biases, one to a partition and block"):
-            nc.scalar.dma_start(b2_sb[:], b2.rearrange("(q p) one -> p (q one)", p=P))
+        x_pieces = [held.tile([P, PIECE], BF16, name=f"x{c}") for c in range(N // PIECE)]
+        nc.sync.dma_start(x_pieces[0][:], x[:, 0:PIECE])
+        nc.gpsimd.dma_start(x_pieces[1][:], x[:, PIECE : 2 * PIECE])
         wb_sb = held.tile([P, P], BF16, name="wb_sb")
-        nc.sync.dma_start(wb_sb[:], wb)
-        bb_sb = held.tile([P, 1], F32, name="bb_sb")
-        nc.scalar.dma_start(bb_sb[:], bb)
-        ones = held.tile([P, P], BF16, name="ones")
+        nc.gpsimd.dma_start(wb_sb[:], wb)
+
+        ones = held.tile([P, PIECE], BF16, name="ones")
         nc.vector.memset(ones[:], 1.0)
+        scratch = held.tile([P, 1], BF16, name="scratch")
+        nc.scalar.activation(scratch[:], ones[:, 0:1], SILU)
+        idle = psum.tile([P, PIECE], F32, name="idle", tag="bank")
+        for i in range(WARM_UP):
+            nc.tensor.matmul(idle[:], ones[:, 0:P], ones[:], start=True, stop=True)
+
+        identity = held.tile([N_BIAS, N_BIAS], F32, name="identity")
+        make_identity(nc, identity[:])
+        bias_ps = psum.tile([P, N_BIAS], F32, name="bias_ps", tag="bank")
+        nc.tensor.matmul(bias_ps[:], bias_rows[:], identity[:], start=True, stop=True)
+        biases = held.tile([P, N_BIAS], F32, name="biases")
+        nc.vector.tensor_copy(biases[:], bias_ps[:])
+        b1_sb = biases[:, 0:1]
+        b2_sb = biases[:, 1 : 1 + 2 * R]
+        bb_sb = biases[:, 1 + 2 * R : N_BIAS]
 
         z_pieces = []
         for c in range(N // PIECE):
@@ -48,35 +66,64 @@ def tile_stylehyperlinear_kernel(tc, styles, w1, b1, w2, b2, x, wb, bb, offs, ou
             nc.tensor.matmul(z[:], w1_sb[:], looked_up, start=True, stop=True)
             z_pieces.append(z)
 
-        for c in range(N // PIECE):
-            cols = slice(c * PIECE, (c + 1) * PIECE)
-            h = work.tile([P, PIECE], BF16, name="h")
-            nc.scalar.activation(h[:], z_pieces[c][:], SILU, bias=b1_sb[:])
+        def chunk_of(pieces, k):
+            return pieces[k * CHUNK // PIECE][:, k * CHUNK % PIECE : k * CHUNK % PIECE + CHUNK]
 
-            p_blocks = []
-            for q in range(2 * R):
-                p_q = psum.tile([P, PIECE], F32, name=f"p{q}", tag="bank")
-                nc.tensor.matmul(p_q[:], w2_sb[:, q * P : (q + 1) * P], h[:], start=True, stop=True)
-                p_blocks.append(p_q)
-            base = psum.tile([P, PIECE], F32, name="base", tag="bank")
-            nc.tensor.matmul(base[:], wb_sb[:], x_sb[:, cols], start=True, stop=True)
+        def hidden(k):
+            h = work.tile([P, CHUNK], BF16, name="h")
+            nc.scalar.activation(h[:], chunk_of(z_pieces, k), SILU, bias=b1_sb)
+            return h
 
-            terms = []
+        def project(h):
+            p_in = psum.tile([P, R * CHUNK], F32, name="p_in", tag="bank")
+            p_out = psum.tile([P, R * CHUNK], F32, name="p_out", tag="bank")
+            for q, p_half in enumerate((p_in, p_in, p_out, p_out)):
+                rank = slice(q % R * CHUNK, (q % R + 1) * CHUNK)
+                nc.tensor.matmul(p_half[:, rank], w2_sb[:, q * P : (q + 1) * P], h[:], start=True, stop=True)
+            return p_in, p_out
+
+        def weigh(k, p_in, p_out):
+            prod = work.tile([P, R * CHUNK], BF16, name="prod")
+            vec = work.tile([P, R * CHUNK], F32, name="vec")
             for r in range(R):
-                prod = work.tile([P, PIECE], BF16, name=f"prod{r}")
+                rank = slice(r * CHUNK, (r + 1) * CHUNK)
                 nc.vector.scalar_tensor_tensor(
-                    prod[:], p_blocks[r][:], b2_sb[:, r : r + 1], x_sb[:, cols], op0=ADD, op1=MULT
+                    prod[:, rank],
+                    p_in[:, rank],
+                    b2_sb[:, r : r + 1],
+                    chunk_of(x_pieces, k),
+                    op0=ADD,
+                    op1=MULT,
                 )
-                low = psum.tile([P, PIECE], F32, name=f"low{r}", tag="bank")
-                nc.tensor.matmul(low[:], ones[:], prod[:], start=True, stop=True)
-                vec = work.tile([P, PIECE], F32, name=f"vec{r}")
-                nc.scalar.activation(vec[:], p_blocks[R + r][:], IDENTITY, bias=b2_sb[:, R + r : R + r + 1])
-                term = work.tile([P, PIECE], F32, name=f"term{r}")
-                nc.vector.tensor_tensor(term[:], low[:], vec[:], MULT)
-                terms.append(term)
+                nc.scalar.activation(vec[:, rank], p_out[:, rank], IDENTITY, bias=b2_sb[:, R + r : R + r + 1])
+            low = psum.tile([P, R * CHUNK], F32, name="low", tag="bank")
+            nc.tensor.matmul(low[:], ones[:, 0:P], prod[:], start=True, stop=True)
+            return low, vec
 
-            part = work.tile([P, PIECE], F32, name="part")
-            nc.vector.scalar_tensor_tensor(part[:], base[:], bb_sb[:], terms[0][:], op0=ADD, op1=ADD)
-            res = work.tile([P, PIECE], F32, name="res")
-            nc.vector.tensor_tensor(res[:], part[:], terms[1][:], ADD)
-            nc.sync.dma_start(out[:, cols], res[:])
+        def finish(k, low, vec):
+            term = work.tile([P, R * CHUNK], F32, name="term")
+            nc.vector.tensor_tensor(term[:], low[:], vec[:], MULT)
+            part = work.tile([P, CHUNK], F32, name="part")
+            nc.vector.scalar_tensor_tensor(
+                part[:], chunk_of(base_pieces, k), bb_sb, term[:, 0:CHUNK], op0=ADD, op1=ADD
+            )
+            res = work.tile([P, CHUNK], F32, name="res")
+            adder = nc.gpsimd if k + 1 < n_chunks else nc.vector
+            adder.tensor_tensor(res[:], part[:], term[:, CHUNK : 2 * CHUNK], ADD)
+            nc.sync.dma_start(out[:, k * CHUNK : (k + 1) * CHUNK], res[:])
+
+        n_chunks = N // CHUNK
+        h_chunks = [hidden(k) for k in range(n_chunks)]
+        p_chunks = {0: project(h_chunks[0]), 1: project(h_chunks[1])}
+        weighed = {0: weigh(0, *p_chunks[0])}
+        base_pieces = []
+        for c in range(N // PIECE):
+            base = psum.tile([P, PIECE], F32, name=f"base{c}", tag="bank")
+            nc.tensor.matmul(base[:], wb_sb[:], x_pieces[c][:], start=True, stop=True)
+            base_pieces.append(base)
+        for k in range(n_chunks):
+            if k + 2 < n_chunks:
+                p_chunks[k + 2] = project(h_chunks[k + 2])
+            if k + 1 < n_chunks:
+                weighed[k + 1] = weigh(k + 1, *p_chunks[k + 1])
+            finish(k, *weighed[k])

@@ -1,14 +1,13 @@
 import concourse.mybir as mybir
-from concourse.masks import make_identity
 
 P = 128
 S = 512
 N = 1024
 R = 2
-PIECE = 512
-CHUNK = 256
-WARM_UP = 4
-N_BIAS = 2 + 2 * R
+PIECE = 256
+N_PIECES = N // PIECE
+WARM_UP = 3
+WARM_COLS = 512
 BF16, F32, U16 = mybir.dt.bfloat16, mybir.dt.float32, mybir.dt.uint16
 ADD, MULT = mybir.AluOpType.add, mybir.AluOpType.mult
 SILU, IDENTITY = mybir.ActivationFunctionType.Silu, mybir.ActivationFunctionType.Identity
@@ -20,110 +19,77 @@ def tile_stylehyperlinear_kernel(tc, styles, w1, b1, w2, b2, x, wb, bb, offs, ou
     nc = tc.nc
     with (
         tc.tile_pool(name="held", bufs=1) as held,
-        tc.tile_pool(name="work", bufs=N // CHUNK) as work,
+        tc.tile_pool(name="work", bufs=N_PIECES) as work,
         tc.psum_pool(name="psum", bufs=8) as psum,
     ):
         offsets = held.tile([P, N // 16], U16, name="offsets")
         nc.sync.dma_start(offsets[:], offs)
-        w1_sb = held.tile([P, P], BF16, name="w1_sb")
-        nc.scalar.dma_start(w1_sb[:], w1)
         bank = held.tile([P, S], BF16, name="bank")
-        nc.sync.dma_start(bank[:], styles)
-        bias_rows = held.tile([N_BIAS, P], F32, name="bias_rows")
-        nc.scalar.dma_start(bias_rows[0:1, :], b1.rearrange("p one -> one p"))
-        nc.scalar.dma_start(bias_rows[1 : 1 + 2 * R, :], b2.rearrange("(q p) one -> q (p one)", p=P))
-        nc.scalar.dma_start(bias_rows[1 + 2 * R : N_BIAS, :], bb.rearrange("p one -> one p"))
+        nc.scalar.dma_start(bank[:], styles)
+        w1_sb = held.tile([P, P], BF16, name="w1_sb")
+        nc.sync.dma_start(w1_sb[:], w1)
+        b1_sb = held.tile([P, 1], F32, name="b1_sb")
+        nc.scalar.dma_start(b1_sb[:], b1)
         w2_sb = held.tile([P, 2 * R * P], BF16, name="w2_sb")
         nc.sync.dma_start(w2_sb[:], w2)
-        x_pieces = [held.tile([P, PIECE], BF16, name=f"x{c}") for c in range(N // PIECE)]
-        nc.sync.dma_start(x_pieces[0][:], x[:, 0:PIECE])
-        nc.gpsimd.dma_start(x_pieces[1][:], x[:, PIECE : 2 * PIECE])
+        b2_sb = held.tile([P, 2 * R], F32, name="b2_sb")
+        with nc.allow_non_contiguous_dma(reason="512 biases, one to a partition and block"):
+            nc.scalar.dma_start(b2_sb[:], b2.rearrange("(q p) one -> p (q one)", p=P))
+        x_sb = held.tile([P, N], BF16, name="x_sb")
+        nc.sync.dma_start(x_sb[:], x)
+        bb_sb = held.tile([P, 1], F32, name="bb_sb")
+        nc.scalar.dma_start(bb_sb[:], bb)
         wb_sb = held.tile([P, P], BF16, name="wb_sb")
         nc.gpsimd.dma_start(wb_sb[:], wb)
 
-        ones = held.tile([P, PIECE], BF16, name="ones")
+        ones = held.tile([P, WARM_COLS], BF16, name="ones")
         nc.vector.memset(ones[:], 1.0)
         scratch = held.tile([P, 1], BF16, name="scratch")
         nc.scalar.activation(scratch[:], ones[:, 0:1], SILU)
-        idle = psum.tile([P, PIECE], F32, name="idle", tag="bank")
+        idle = psum.tile([P, WARM_COLS], F32, name="idle", tag="bank")
         for i in range(WARM_UP):
             nc.tensor.matmul(idle[:], ones[:, 0:P], ones[:], start=True, stop=True)
 
-        identity = held.tile([N_BIAS, N_BIAS], F32, name="identity")
-        make_identity(nc, identity[:])
-        bias_ps = psum.tile([P, N_BIAS], F32, name="bias_ps", tag="bank")
-        nc.tensor.matmul(bias_ps[:], bias_rows[:], identity[:], start=True, stop=True)
-        biases = held.tile([P, N_BIAS], F32, name="biases")
-        nc.vector.tensor_copy(biases[:], bias_ps[:])
-        b1_sb = biases[:, 0:1]
-        b2_sb = biases[:, 1 : 1 + 2 * R]
-        bb_sb = biases[:, 1 + 2 * R : N_BIAS]
+        def bank_tile(name, columns):
+            return psum.tile([P, columns], F32, name=name, tag="bank")
 
-        z_pieces = []
-        for c in range(N // PIECE):
-            z = psum.tile([P, PIECE], F32, name=f"z{c}", tag="bank")
+
+        z = [bank_tile(f"z{c}", PIECE) for c in range(N_PIECES)]
+        for c in range(N_PIECES):
             looked_up = bank[:].indirect(offsets[:, c * (PIECE // 16) : (c + 1) * (PIECE // 16)])
-            nc.tensor.matmul(z[:], w1_sb[:], looked_up, start=True, stop=True)
-            z_pieces.append(z)
+            nc.tensor.matmul(z[c][:], w1_sb[:], looked_up, start=True, stop=True)
 
-        def chunk_of(pieces, k):
-            return pieces[k * CHUNK // PIECE][:, k * CHUNK % PIECE : k * CHUNK % PIECE + CHUNK]
+        h = [work.tile([P, PIECE], BF16, name="h") for c in range(N_PIECES)]
+        for c in range(N_PIECES):
+            nc.scalar.activation(h[c][:], z[c][:], SILU, bias=b1_sb[:])
 
-        def hidden(k):
-            h = work.tile([P, CHUNK], BF16, name="h")
-            nc.scalar.activation(h[:], chunk_of(z_pieces, k), SILU, bias=b1_sb)
-            return h
+        p = [[bank_tile(f"p{q}", PIECE) for q in range(2 * R)] for c in range(N_PIECES)]
+        for c in range(N_PIECES):
+            for q in range(2 * R):
+                nc.tensor.matmul(p[c][q][:], w2_sb[:, q * P : (q + 1) * P], h[c][:], start=True, stop=True)
 
-        def project(h):
-            p_in = psum.tile([P, R * CHUNK], F32, name="p_in", tag="bank")
-            p_out = psum.tile([P, R * CHUNK], F32, name="p_out", tag="bank")
-            for q, p_half in enumerate((p_in, p_in, p_out, p_out)):
-                rank = slice(q % R * CHUNK, (q % R + 1) * CHUNK)
-                nc.tensor.matmul(p_half[:, rank], w2_sb[:, q * P : (q + 1) * P], h[:], start=True, stop=True)
-            return p_in, p_out
-
-        def weigh(k, p_in, p_out):
-            prod = work.tile([P, R * CHUNK], BF16, name="prod")
-            vec = work.tile([P, R * CHUNK], F32, name="vec")
+        low, vec, base = [], [], []
+        for c in range(N_PIECES):
+            cols = slice(c * PIECE, (c + 1) * PIECE)
+            prod = work.tile([P, R * PIECE], BF16, name="prod")
+            vec.append(work.tile([P, R * PIECE], F32, name="vec"))
             for r in range(R):
-                rank = slice(r * CHUNK, (r + 1) * CHUNK)
+                rank = slice(r * PIECE, (r + 1) * PIECE)
                 nc.vector.scalar_tensor_tensor(
-                    prod[:, rank],
-                    p_in[:, rank],
-                    b2_sb[:, r : r + 1],
-                    chunk_of(x_pieces, k),
-                    op0=ADD,
-                    op1=MULT,
+                    prod[:, rank], p[c][r][:], b2_sb[:, r : r + 1], x_sb[:, cols], op0=ADD, op1=MULT
                 )
-                nc.scalar.activation(vec[:, rank], p_out[:, rank], IDENTITY, bias=b2_sb[:, R + r : R + r + 1])
-            low = psum.tile([P, R * CHUNK], F32, name="low", tag="bank")
-            nc.tensor.matmul(low[:], ones[:, 0:P], prod[:], start=True, stop=True)
-            return low, vec
+                nc.scalar.activation(vec[c][:, rank], p[c][R + r][:], IDENTITY, bias=b2_sb[:, R + r : R + r + 1])
+            low.append(bank_tile("low", R * PIECE))
+            nc.tensor.matmul(low[c][:], ones[:, 0:P], prod[:], start=True, stop=True)
+            base.append(bank_tile("base", PIECE))
+            nc.tensor.matmul(base[c][:], wb_sb[:], x_sb[:, cols], start=True, stop=True)
 
-        def finish(k, low, vec):
-            term = work.tile([P, R * CHUNK], F32, name="term")
-            nc.vector.tensor_tensor(term[:], low[:], vec[:], MULT)
-            part = work.tile([P, CHUNK], F32, name="part")
-            nc.vector.scalar_tensor_tensor(
-                part[:], chunk_of(base_pieces, k), bb_sb, term[:, 0:CHUNK], op0=ADD, op1=ADD
-            )
-            res = work.tile([P, CHUNK], F32, name="res")
-            adder = nc.gpsimd if k + 1 < n_chunks else nc.vector
-            adder.tensor_tensor(res[:], part[:], term[:, CHUNK : 2 * CHUNK], ADD)
-            nc.sync.dma_start(out[:, k * CHUNK : (k + 1) * CHUNK], res[:])
-
-        n_chunks = N // CHUNK
-        h_chunks = [hidden(k) for k in range(n_chunks)]
-        p_chunks = {0: project(h_chunks[0]), 1: project(h_chunks[1])}
-        weighed = {0: weigh(0, *p_chunks[0])}
-        base_pieces = []
-        for c in range(N // PIECE):
-            base = psum.tile([P, PIECE], F32, name=f"base{c}", tag="bank")
-            nc.tensor.matmul(base[:], wb_sb[:], x_pieces[c][:], start=True, stop=True)
-            base_pieces.append(base)
-        for k in range(n_chunks):
-            if k + 2 < n_chunks:
-                p_chunks[k + 2] = project(h_chunks[k + 2])
-            if k + 1 < n_chunks:
-                weighed[k + 1] = weigh(k + 1, *p_chunks[k + 1])
-            finish(k, *weighed[k])
+        for c in range(N_PIECES):
+            term = work.tile([P, R * PIECE], F32, name="term")
+            nc.vector.tensor_tensor(term[:], low[c][:], vec[c][:], MULT)
+            part = work.tile([P, PIECE], F32, name="part")
+            nc.vector.scalar_tensor_tensor(part[:], base[c][:], bb_sb[:], term[:, 0:PIECE], op0=ADD, op1=ADD)
+            res = work.tile([P, PIECE], F32, name="res")
+            adder = nc.gpsimd if c + 1 < N_PIECES else nc.vector
+            adder.tensor_tensor(res[:], part[:], term[:, PIECE : 2 * PIECE], ADD)
+            nc.sync.dma_start(out[:, c * PIECE : (c + 1) * PIECE], res[:])

@@ -6,8 +6,6 @@ N = 1024
 R = 2
 PIECE = 256
 N_PIECES = N // PIECE
-WARM_UP = 3
-WARM_COLS = 512
 BF16, F32, U16 = mybir.dt.bfloat16, mybir.dt.float32, mybir.dt.uint16
 ADD, MULT = mybir.AluOpType.add, mybir.AluOpType.mult
 SILU, IDENTITY = mybir.ActivationFunctionType.Silu, mybir.ActivationFunctionType.Identity
@@ -42,13 +40,10 @@ def tile_stylehyperlinear_kernel(tc, styles, w1, b1, w2, b2, x, wb, bb, offs, ou
         wb_sb = held.tile([P, P], BF16, name="wb_sb")
         nc.gpsimd.dma_start(wb_sb[:], wb)
 
-        ones = held.tile([P, WARM_COLS], BF16, name="ones")
+        ones = held.tile([P, P], BF16, name="ones")
         nc.vector.memset(ones[:], 1.0)
         scratch = held.tile([P, 1], BF16, name="scratch")
         nc.scalar.activation(scratch[:], ones[:, 0:1], SILU)
-        idle = psum.tile([P, WARM_COLS], F32, name="idle", tag="bank")
-        for i in range(WARM_UP):
-            nc.tensor.matmul(idle[:], ones[:, 0:P], ones[:], start=True, stop=True)
 
         def bank_tile(name, columns):
             return psum.tile([P, columns], F32, name=name, tag="bank")

@@ -6,6 +6,8 @@ N = 1024
 R = 2
 PIECE = 256
 N_PIECES = N // PIECE
+WARM_UP = 3
+WARM_COLS = 512
 BF16, F32, U16 = mybir.dt.bfloat16, mybir.dt.float32, mybir.dt.uint16
 ADD, MULT = mybir.AluOpType.add, mybir.AluOpType.mult
 SILU, IDENTITY = mybir.ActivationFunctionType.Silu, mybir.ActivationFunctionType.Identity
@@ -40,10 +42,11 @@ def tile_stylehyperlinear_kernel(tc, styles, w1, b1, w2, b2, x, wb, bb, offs, ou
         wb_sb = held.tile([P, P], BF16, name="wb_sb")
         nc.gpsimd.dma_start(wb_sb[:], wb)
 
-        ones = held.tile([P, P], BF16, name="ones")
+        ones = held.tile([P, WARM_COLS], BF16, name="ones")
         nc.vector.memset(ones[:], 1.0)
-        scratch = held.tile([P, 1], BF16, name="scratch")
-        nc.scalar.activation(scratch[:], ones[:, 0:1], SILU)
+        idle = psum.tile([P, WARM_COLS], F32, name="idle", tag="bank")
+        for i in range(WARM_UP):
+            nc.tensor.matmul(idle[:], ones[:, 0:P], ones[:], start=True, stop=True)
 
         def bank_tile(name, columns):
             return psum.tile([P, columns], F32, name=name, tag="bank")

@@ -35,15 +35,18 @@ def tile_stylehyperlinear_kernel(tc, styles, w1, b1, w2, b2, x, wb, bb, offs, ou
         b2_sb = held.tile([P, 2 * R], F32, name="b2_sb")
         with nc.allow_non_contiguous_dma(reason="512 biases, one to a partition and block"):
             nc.scalar.dma_start(b2_sb[:], b2.rearrange("(q p) one -> p (q one)", p=P))
-        x_sb = held.tile([P, N], BF16, name="x_sb")
-        nc.sync.dma_start(x_sb[:], x)
+        x_half = [held.tile([P, N // 2], BF16, name=f"x_half{i}") for i in range(2)]
+        nc.sync.dma_start(x_half[0][:], x[:, 0 : N // 2])
         bb_sb = held.tile([P, 1], F32, name="bb_sb")
         nc.scalar.dma_start(bb_sb[:], bb)
+        nc.gpsimd.dma_start(x_half[1][:], x[:, N // 2 : N])
         wb_sb = held.tile([P, P], BF16, name="wb_sb")
         nc.gpsimd.dma_start(wb_sb[:], wb)
 
         ones = held.tile([P, WARM_COLS], BF16, name="ones")
         nc.vector.memset(ones[:], 1.0)
+        scratch = held.tile([P, 1], BF16, name="scratch")
+        nc.scalar.activation(scratch[:], ones[:, 0:1], SILU)
         idle = psum.tile([P, WARM_COLS], F32, name="idle", tag="bank")
         for i in range(WARM_UP):
             nc.tensor.matmul(idle[:], ones[:, 0:P], ones[:], start=True, stop=True)
@@ -68,19 +71,19 @@ def tile_stylehyperlinear_kernel(tc, styles, w1, b1, w2, b2, x, wb, bb, offs, ou
 
         low, vec, base = [], [], []
         for c in range(N_PIECES):
-            cols = slice(c * PIECE, (c + 1) * PIECE)
+            x_piece = x_half[c * PIECE // (N // 2)][:, c * PIECE % (N // 2) : c * PIECE % (N // 2) + PIECE]
             prod = work.tile([P, R * PIECE], BF16, name="prod")
             vec.append(work.tile([P, R * PIECE], F32, name="vec"))
             for r in range(R):
                 rank = slice(r * PIECE, (r + 1) * PIECE)
                 nc.vector.scalar_tensor_tensor(
-                    prod[:, rank], p[c][r][:], b2_sb[:, r : r + 1], x_sb[:, cols], op0=ADD, op1=MULT
+                    prod[:, rank], p[c][r][:], b2_sb[:, r : r + 1], x_piece, op0=ADD, op1=MULT
                 )
                 nc.scalar.activation(vec[c][:, rank], p[c][R + r][:], IDENTITY, bias=b2_sb[:, R + r : R + r + 1])
             low.append(bank_tile("low", R * PIECE))
             nc.tensor.matmul(low[c][:], ones[:, 0:P], prod[:], start=True, stop=True)
             base.append(bank_tile("base", PIECE))
-            nc.tensor.matmul(base[c][:], wb_sb[:], x_sb[:, cols], start=True, stop=True)
+            nc.tensor.matmul(base[c][:], wb_sb[:], x_piece, start=True, stop=True)
 
         for c in range(N_PIECES):
             term = work.tile([P, R * PIECE], F32, name="term")

@@ -1,4 +1,5 @@
 import concourse.mybir as mybir
+from concourse.masks import make_identity
 
 P = 128
 S = 512
@@ -47,13 +48,14 @@ def tile_stylehyperlinear_kernel(tc, styles, w1, b1, w2, b2, x, wb, bb, offs, ou
         nc.vector.memset(ones[:], 1.0)
         scratch = held.tile([P, 1], BF16, name="scratch")
         nc.scalar.activation(scratch[:], ones[:, 0:1], SILU)
+        identity = held.tile([P, P], F32, name="identity")
+        make_identity(nc, identity[:])
         idle = psum.tile([P, WARM_COLS], F32, name="idle", tag="bank")
         for i in range(WARM_UP):
             nc.tensor.matmul(idle[:], ones[:, 0:P], ones[:], start=True, stop=True)
 
         def bank_tile(name, columns):
             return psum.tile([P, columns], F32, name=name, tag="bank")
-
 
         z = [bank_tile(f"z{c}", PIECE) for c in range(N_PIECES)]
         for c in range(N_PIECES):
@@ -64,33 +66,64 @@ def tile_stylehyperlinear_kernel(tc, styles, w1, b1, w2, b2, x, wb, bb, offs, ou
         for c in range(N_PIECES):
             nc.scalar.activation(h[c][:], z[c][:], SILU, bias=b1_sb[:])
 
-        p = [[bank_tile(f"p{q}", PIECE) for q in range(2 * R)] for c in range(N_PIECES)]
-        for c in range(N_PIECES):
-            for q in range(2 * R):
-                nc.tensor.matmul(p[c][q][:], w2_sb[:, q * P : (q + 1) * P], h[c][:], start=True, stop=True)
+        def ranks():
+            return [(r, slice(r * PIECE, (r + 1) * PIECE)) for r in range(R)]
 
-        low, vec, base = [], [], []
-        for c in range(N_PIECES):
-            x_piece = x_half[c * PIECE // (N // 2)][:, c * PIECE % (N // 2) : c * PIECE % (N // 2) + PIECE]
-            prod = work.tile([P, R * PIECE], BF16, name="prod")
-            vec.append(work.tile([P, R * PIECE], F32, name="vec"))
-            for r in range(R):
-                rank = slice(r * PIECE, (r + 1) * PIECE)
+        def x_piece(c):
+            return x_half[c * PIECE // (N // 2)][:, c * PIECE % (N // 2) : c * PIECE % (N // 2) + PIECE]
+
+        prod, vec, low, base, base_sb = {}, {}, {}, {}, {}
+
+        summer = ["vector" if c >= N_PIECES // 2 else "gpsimd" if c % 2 == 0 else "tensor" for c in range(N_PIECES)]
+
+        def input_vectors(c):
+            p_in = bank_tile("p_in", R * PIECE)
+            prod[c] = work.tile([P, R * PIECE], BF16, name="prod")
+            for r, rank in ranks():
+                nc.tensor.matmul(p_in[:, rank], w2_sb[:, r * P : (r + 1) * P], h[c][:], start=True, stop=True)
+            for r, rank in ranks():
                 nc.vector.scalar_tensor_tensor(
-                    prod[:, rank], p[c][r][:], b2_sb[:, r : r + 1], x_piece, op0=ADD, op1=MULT
+                    prod[c][:, rank], p_in[:, rank], b2_sb[:, r : r + 1], x_piece(c), op0=ADD, op1=MULT
                 )
-                nc.scalar.activation(vec[c][:, rank], p[c][R + r][:], IDENTITY, bias=b2_sb[:, R + r : R + r + 1])
-            low.append(bank_tile("low", R * PIECE))
-            nc.tensor.matmul(low[c][:], ones[:, 0:P], prod[:], start=True, stop=True)
-            base.append(bank_tile("base", PIECE))
-            nc.tensor.matmul(base[c][:], wb_sb[:], x_piece, start=True, stop=True)
 
-        for c in range(N_PIECES):
+        def output_vectors(c):
+            p_out = bank_tile("p_out", R * PIECE)
+            vec[c] = work.tile([P, R * PIECE], F32, name="vec")
+            for r, rank in ranks():
+                nc.tensor.matmul(p_out[:, rank], w2_sb[:, (R + r) * P : (R + r + 1) * P], h[c][:], start=True, stop=True)
+            for r, rank in ranks():
+                nc.scalar.activation(vec[c][:, rank], p_out[:, rank], IDENTITY, bias=b2_sb[:, R + r : R + r + 1])
+
+        def sums_over_features(c):
+            low[c] = bank_tile("low", R * PIECE)
+            nc.tensor.matmul(low[c][:], ones[:, 0:P], prod[c][:], start=True, stop=True)
+            base[c] = bank_tile("base", PIECE)
+            nc.tensor.matmul(base[c][:], wb_sb[:], x_piece(c), start=True, stop=summer[c] != "tensor")
+            if summer[c] == "gpsimd":
+                base_sb[c] = work.tile([P, PIECE], F32, name="base_sb")
+                nc.scalar.activation(base_sb[c][:], base[c][:], IDENTITY, bias=bb_sb[:])
+
+        def finish(c):
             term = work.tile([P, R * PIECE], F32, name="term")
             nc.vector.tensor_tensor(term[:], low[c][:], vec[c][:], MULT)
-            part = work.tile([P, PIECE], F32, name="part")
-            nc.vector.scalar_tensor_tensor(part[:], base[c][:], bb_sb[:], term[:, 0:PIECE], op0=ADD, op1=ADD)
             res = work.tile([P, PIECE], F32, name="res")
-            adder = nc.gpsimd if c + 1 < N_PIECES else nc.vector
-            adder.tensor_tensor(res[:], part[:], term[:, PIECE : 2 * PIECE], ADD)
+            if summer[c] == "tensor":
+                for r, rank in ranks():
+                    nc.tensor.matmul(base[c][:], identity[:], term[:, rank], start=False, stop=r == R - 1)
+                nc.scalar.activation(res[:], base[c][:], IDENTITY, bias=bb_sb[:])
+            elif summer[c] == "gpsimd":
+                delta = work.tile([P, PIECE], F32, name="delta")
+                nc.gpsimd.tensor_tensor(delta[:], term[:, 0:PIECE], term[:, PIECE : 2 * PIECE], ADD)
+                nc.gpsimd.tensor_tensor(res[:], delta[:], base_sb[c][:], ADD)
+            else:
+                part = work.tile([P, PIECE], F32, name="part")
+                nc.vector.scalar_tensor_tensor(part[:], base[c][:], bb_sb[:], term[:, 0:PIECE], op0=ADD, op1=ADD)
+                adder = nc.gpsimd if c + 1 < N_PIECES else nc.vector
+                adder.tensor_tensor(res[:], part[:], term[:, PIECE : 2 * PIECE], ADD)
             nc.sync.dma_start(out[:, c * PIECE : (c + 1) * PIECE], res[:])
+
+        stages = [input_vectors, output_vectors, sums_over_features, finish]
+        for step in range(N_PIECES + len(stages) - 1):
+            for behind, stage in enumerate(stages):
+                if 0 <= step - behind < N_PIECES:
+                    stage(step - behind)

@@ -77,14 +77,18 @@ def tile_stylehyperlinear_kernel(tc, styles, w1, b1, w2, b2, x, wb, bb, offs, ou
         summer = ["vector" if c >= N_PIECES // 2 else "gpsimd" if c % 2 == 0 else "tensor" for c in range(N_PIECES)]
 
         def input_vectors(c):
-            p_in = bank_tile("p_in", R * PIECE)
             prod[c] = work.tile([P, R * PIECE], BF16, name="prod")
             for r, rank in ranks():
-                nc.tensor.matmul(p_in[:, rank], w2_sb[:, r * P : (r + 1) * P], h[c][:], start=True, stop=True)
-            for r, rank in ranks():
-                nc.vector.scalar_tensor_tensor(
-                    prod[c][:, rank], p_in[:, rank], b2_sb[:, r : r + 1], x_piece(c), op0=ADD, op1=MULT
-                )
+                p_in = bank_tile(f"p_in{r}", PIECE)
+                nc.tensor.matmul(p_in[:], w2_sb[:, r * P : (r + 1) * P], h[c][:], start=True, stop=True)
+                if r == R - 1 and 0 < c < N_PIECES - 1:
+                    moved = work.tile([P, PIECE], F32, name="moved")
+                    nc.scalar.activation(moved[:], p_in[:], IDENTITY, bias=b2_sb[:, r : r + 1])
+                    nc.gpsimd.tensor_tensor(prod[c][:, rank], moved[:], x_piece(c), MULT)
+                else:
+                    nc.vector.scalar_tensor_tensor(
+                        prod[c][:, rank], p_in[:], b2_sb[:, r : r + 1], x_piece(c), op0=ADD, op1=MULT
+                    )
 
         def output_vectors(c):
             p_out = bank_tile("p_out", R * PIECE)

import concourse.mybir as mybir
from concourse.masks import make_identity

P = 128
S = 512
N = 1024
R = 2
PIECE = 256
N_PIECES = N // PIECE
WARM_UP = 3
WARM_COLS = 512
BF16, F32, U16 = mybir.dt.bfloat16, mybir.dt.float32, mybir.dt.uint16
ADD, MULT = mybir.AluOpType.add, mybir.AluOpType.mult
SILU, IDENTITY = mybir.ActivationFunctionType.Silu, mybir.ActivationFunctionType.Identity

FLOPS = 2 * N * (P * P + P * 2 * R * P + P * P) + 4 * R * P * N


def tile_stylehyperlinear_kernel(tc, styles, w1, b1, w2, b2, x, wb, bb, offs, out):
    nc = tc.nc
    with (
        tc.tile_pool(name="held", bufs=1) as held,
        tc.tile_pool(name="work", bufs=N_PIECES) as work,
        tc.psum_pool(name="psum", bufs=8) as psum,
    ):
        offsets = held.tile([P, N // 16], U16, name="offsets")
        nc.sync.dma_start(offsets[:], offs)
        bank = held.tile([P, S], BF16, name="bank")
        nc.scalar.dma_start(bank[:], styles)
        w1_sb = held.tile([P, P], BF16, name="w1_sb")
        nc.sync.dma_start(w1_sb[:], w1)
        b1_sb = held.tile([P, 1], F32, name="b1_sb")
        nc.scalar.dma_start(b1_sb[:], b1)
        w2_sb = held.tile([P, 2 * R * P], BF16, name="w2_sb")
        nc.sync.dma_start(w2_sb[:], w2)
        b2_sb = held.tile([P, 2 * R], F32, name="b2_sb")
        with nc.allow_non_contiguous_dma(reason="512 biases, one to a partition and block"):
            nc.scalar.dma_start(b2_sb[:], b2.rearrange("(q p) one -> p (q one)", p=P))
        x_half = [held.tile([P, N // 2], BF16, name=f"x_half{i}") for i in range(2)]
        nc.sync.dma_start(x_half[0][:], x[:, 0 : N // 2])
        bb_sb = held.tile([P, 1], F32, name="bb_sb")
        nc.scalar.dma_start(bb_sb[:], bb)
        nc.gpsimd.dma_start(x_half[1][:], x[:, N // 2 : N])
        wb_sb = held.tile([P, P], BF16, name="wb_sb")
        nc.gpsimd.dma_start(wb_sb[:], wb)

        ones = held.tile([P, WARM_COLS], BF16, name="ones")
        nc.vector.memset(ones[:], 1.0)
        scratch = held.tile([P, 1], BF16, name="scratch")
        nc.scalar.activation(scratch[:], ones[:, 0:1], SILU)
        identity = held.tile([P, P], F32, name="identity")
        make_identity(nc, identity[:])
        idle = psum.tile([P, WARM_COLS], F32, name="idle", tag="bank")
        for i in range(WARM_UP):
            nc.tensor.matmul(idle[:], ones[:, 0:P], ones[:], start=True, stop=True)

        def bank_tile(name, columns):
            return psum.tile([P, columns], F32, name=name, tag="bank")

        z = [bank_tile(f"z{c}", PIECE) for c in range(N_PIECES)]
        for c in range(N_PIECES):
            looked_up = bank[:].indirect(offsets[:, c * (PIECE // 16) : (c + 1) * (PIECE // 16)])
            nc.tensor.matmul(z[c][:], w1_sb[:], looked_up, start=True, stop=True)

        h = [work.tile([P, PIECE], BF16, name="h") for c in range(N_PIECES)]
        for c in range(N_PIECES):
            nc.scalar.activation(h[c][:], z[c][:], SILU, bias=b1_sb[:])

        def ranks():
            return [(r, slice(r * PIECE, (r + 1) * PIECE)) for r in range(R)]

        def x_piece(c):
            return x_half[c * PIECE // (N // 2)][:, c * PIECE % (N // 2) : c * PIECE % (N // 2) + PIECE]

        prod, vec, low, base, base_sb = {}, {}, {}, {}, {}

        summer = ["vector" if c >= N_PIECES // 2 else "gpsimd" if c % 2 == 0 else "tensor" for c in range(N_PIECES)]

        def input_vectors(c):
            prod[c] = work.tile([P, R * PIECE], BF16, name="prod")
            for r, rank in ranks():
                p_in = bank_tile(f"p_in{r}", PIECE)
                nc.tensor.matmul(p_in[:], w2_sb[:, r * P : (r + 1) * P], h[c][:], start=True, stop=True)
                if r == R - 1 and 0 < c < N_PIECES - 1:
                    moved = work.tile([P, PIECE], F32, name="moved")
                    nc.scalar.activation(moved[:], p_in[:], IDENTITY, bias=b2_sb[:, r : r + 1])
                    nc.gpsimd.tensor_tensor(prod[c][:, rank], moved[:], x_piece(c), MULT)
                else:
                    nc.vector.scalar_tensor_tensor(
                        prod[c][:, rank], p_in[:], b2_sb[:, r : r + 1], x_piece(c), op0=ADD, op1=MULT
                    )

        def output_vectors(c):
            p_out = bank_tile("p_out", R * PIECE)
            vec[c] = work.tile([P, R * PIECE], F32, name="vec")
            for r, rank in ranks():
                nc.tensor.matmul(p_out[:, rank], w2_sb[:, (R + r) * P : (R + r + 1) * P], h[c][:], start=True, stop=True)
            for r, rank in ranks():
                nc.scalar.activation(vec[c][:, rank], p_out[:, rank], IDENTITY, bias=b2_sb[:, R + r : R + r + 1])

        def sums_over_features(c):
            low[c] = bank_tile("low", R * PIECE)
            nc.tensor.matmul(low[c][:], ones[:, 0:P], prod[c][:], start=True, stop=True)
            base[c] = bank_tile("base", PIECE)
            nc.tensor.matmul(base[c][:], wb_sb[:], x_piece(c), start=True, stop=summer[c] != "tensor")
            if summer[c] == "gpsimd":
                base_sb[c] = work.tile([P, PIECE], F32, name="base_sb")
                nc.scalar.activation(base_sb[c][:], base[c][:], IDENTITY, bias=bb_sb[:])

        def finish(c):
            term = work.tile([P, R * PIECE], F32, name="term")
            nc.vector.tensor_tensor(term[:], low[c][:], vec[c][:], MULT)
            res = work.tile([P, PIECE], F32, name="res")
            if summer[c] == "tensor":
                for r, rank in ranks():
                    nc.tensor.matmul(base[c][:], identity[:], term[:, rank], start=False, stop=r == R - 1)
                nc.scalar.activation(res[:], base[c][:], IDENTITY, bias=bb_sb[:])
            elif summer[c] == "gpsimd":
                delta = work.tile([P, PIECE], F32, name="delta")
                nc.gpsimd.tensor_tensor(delta[:], term[:, 0:PIECE], term[:, PIECE : 2 * PIECE], ADD)
                nc.gpsimd.tensor_tensor(res[:], delta[:], base_sb[c][:], ADD)
            else:
                part = work.tile([P, PIECE], F32, name="part")
                nc.vector.scalar_tensor_tensor(part[:], base[c][:], bb_sb[:], term[:, 0:PIECE], op0=ADD, op1=ADD)
                adder = nc.gpsimd if c + 1 < N_PIECES else nc.vector
                adder.tensor_tensor(res[:], part[:], term[:, PIECE : 2 * PIECE], ADD)
            nc.sync.dma_start(out[:, c * PIECE : (c + 1) * PIECE], res[:])

        stages = [input_vectors, output_vectors, sums_over_features, finish]
        for step in range(N_PIECES + len(stages) - 1):
            for behind, stage in enumerate(stages):
                if 0 <= step - behind < N_PIECES:
                    stage(step - behind)
